import numpy as np
import ml_dtypes


def mxq(x, axis, fmt="e4m3"):
    dtype, down = {"e4m3": (ml_dtypes.float8_e4m3fn, 7), "e5m2": (ml_dtypes.float8_e5m2, 14)}[fmt]
    v = np.moveaxis(np.asarray(x, np.float32).astype(ml_dtypes.bfloat16).astype(np.float64), axis, -1)
    blocks = v.reshape(v.shape[:-1] + (-1, 32))
    amax = np.abs(blocks).max(-1, keepdims=True)
    byte = np.maximum(np.where(amax > 0, np.frexp(amax)[1] - 1 + 127, 0) - down, 1)
    scale = np.exp2(byte - 127.0)
    codes = (blocks / scale).astype(np.float32).astype(dtype).astype(np.float64)
    return np.moveaxis((codes * scale).reshape(v.shape), -1, axis)


WIDE = False


def mx_kscale(k):
    if not WIDE:
        return np.ones(k)
    levels = np.array([10, -10, 5, -5, 0])
    if k % 512:
        return np.exp2(np.random.permutation(np.resize(levels, k // 32))).repeat(32)
    a = np.empty((k // 512, 16))
    for p in range(k // 512):
        a[p, :8] = np.random.permutation(np.resize(levels, 8))
        for g in range(8):
            far = levels[np.abs(levels - a[p, g]) >= 10]
            a[p, g + 8] = far[np.random.randint(len(far))]
    return np.exp2(a.ravel()).repeat(32)


BF16 = ml_dtypes.bfloat16


def bf(x):
    return np.asarray(x, np.float32).astype(BF16)


def f64(x):
    return np.asarray(x).astype(np.float64)


B, N, D, P, Z = 1, 128, 1024, 511, 32
P1 = P + 1


def leaky_draw(shape):
    g = np.random.standard_normal(shape)
    return np.where(g > 0.0, g, 0.1 * g)


def with_ones(v):
    return np.concatenate([v, np.ones(v.shape[:-1] + (1,))], axis=-1)


def setup_inputs():
    s, u = mx_kscale(P1), mx_kscale(P1)
    s, u = s / s[-1], u / u[-1]
    return {"xp": bf(leaky_draw((B, N, P)) * s[:P]),
            "yp": bf(leaky_draw((B, N, P)) / u[:P]),
            "w": bf(np.random.standard_normal((B, Z, P1, P1)) * 0.36 / np.sqrt(P1) / s[:, None] * u)}


def reference(xp, yp, w):
    x1 = mxq(with_ones(f64(xp)), 2, "e4m3")
    y1 = mxq(with_ones(f64(yp)), 2, "e4m3")
    t = x1[:, None] @ mxq(f64(w), 2, "e4m3")
    sc = mxq(t, 3, "e4m3") @ y1.transpose(0, 2, 1)[:, None]
    return sc.transpose(0, 2, 3, 1)

@@ -1,0 +1,179 @@
+from contextlib import ExitStack
+
+import concourse.masks as masks
+import concourse.mybir as mybir
+
+BF16 = mybir.dt.bfloat16
+F32 = mybir.dt.float32
+U32 = mybir.dt.uint32
+U8 = mybir.dt.uint8
+FP8X4 = mybir.dt.float8_e4m3fn_x4
+
+P = 128
+PACK = 4
+K = P * PACK
+N_MAPS = 32
+GROUP = 4
+N_GROUPS = N_MAPS // GROUP
+
+FLOPS = 2 * N_MAPS * P * K * K + 2 * N_MAPS * P * P * K
+
+RUN = 8
+N_BLOCKS = K // (PACK * RUN)
+VECTOR_BLOCKS = 10
+
+ROUND_LAG = 2
+SECOND_LAG = 15
+GATHER_LAG = 17
+
+STORE_CHUNKS = 4
+
+
+def load_with_ones(nc, pool, feats, name):
+    full = pool.tile([P, K], BF16, name=name)
+    nc.vector.memset(full[:, K - 16 : K], 1.0)
+    nc.scalar.dma_start(out=full[:, 0 : K - 1], in_=feats.rearrange("b n f -> (b n) f"))
+    return full
+
+
+def transpose_and_quantise(nc, psum, pool, planes, ident, name):
+    turned = psum.tile([P, PACK, P], BF16, name="turned", tag="t_bank")
+    for t in range(PACK):
+        nc.tensor.transpose(turned[:, t, :], planes[:, t, :], ident[:])
+    grouped = pool.tile([P, P, PACK], BF16, name=name + "_grouped", align_bytes=64)
+    nc.scalar.copy(out=grouped[:], in_=turned[:].rearrange("p t n -> p n t"))
+    codes = pool.tile([P, P], U32, name=name + "_codes", align_bytes=64)
+    scales = pool.tile([P, P], U8, name=name + "_scales", align_bytes=64)
+    nc.vector.quantize_mx(
+        out=codes[:].bitcast(FP8X4),
+        scales=scales[:],
+        in_=grouped[:].rearrange("p n t -> p (n t)"),
+    )
+    return codes, scales
+
+
+def tile_span2oscorer_pa_kernel(tc, xp, yp, w, out):
+    nc = tc.nc
+    with ExitStack() as ctx:
+        keep = ctx.enter_context(tc.tile_pool(name="keep", bufs=1))
+        raw_pool = ctx.enter_context(tc.tile_pool(name="raw", bufs=N_MAPS))
+        map_pool = ctx.enter_context(tc.tile_pool(name="map", bufs=4))
+        t_pool = ctx.enter_context(tc.tile_pool(name="t", bufs=6))
+        psum_t = ctx.enter_context(tc.psum_pool(name="psum_t", bufs=4))
+        psum_out = ctx.enter_context(tc.psum_pool(name="psum_out", bufs=4))
+
+        raw = []
+        for z in range(N_MAPS):
+            raw_z = raw_pool.tile([P, PACK, K], BF16, name="raw_z")
+            nc.sync.dma_start(out=raw_z[:], in_=w[0, z].rearrange("(p t) j -> p t j", t=PACK))
+            raw.append(raw_z)
+        x1 = load_with_ones(nc, keep, xp, "x1")
+        y1 = load_with_ones(nc, keep, yp, "y1")
+
+        ident = keep.tile([P, P], BF16, name="ident")
+        masks.make_identity(nc, ident[:])
+        out_sb = keep.tile([P, P, N_MAPS], F32, name="out_sb")
+        out_rows = out.rearrange("b x y z -> (b x) y z")
+
+        map_grouped = {}
+        t_bank = {}
+        t_grouped = {}
+        out_bank = {}
+
+        def regroup(z):
+            grouped = map_pool.tile([P, K, PACK], BF16, name="map_grouped", align_bytes=64)
+            src = raw[z][:].rearrange("p t (q b r) -> p q b t r", b=PACK, r=RUN)
+            dst = grouped[:].rearrange("p (b q r) t -> p q b t r", b=PACK, r=RUN)
+            nc.vector.tensor_copy(out=dst[:, :VECTOR_BLOCKS], in_=src[:, :VECTOR_BLOCKS])
+            nc.scalar.copy(out=dst[:, VECTOR_BLOCKS:], in_=src[:, VECTOR_BLOCKS:])
+            map_grouped[z] = grouped
+
+        def first_product(z):
+            codes = map_pool.tile([P, K], U32, name="map_codes", align_bytes=64)
+            scales = map_pool.tile([P, K], U8, name="map_scales", align_bytes=64)
+            nc.vector.quantize_mx(
+                out=codes[:].bitcast(FP8X4),
+                scales=scales[:],
+                in_=map_grouped[z][:].rearrange("p j t -> p (j t)"),
+            )
+            bank = psum_t.tile([P, PACK, P], F32, name="t_bank")
+            for b in range(PACK):
+                j_cols = slice(b * P, (b + 1) * P)
+                nc.tensor.matmul_mx(
+                    out=bank[:, b, :],
+                    lhsT=codes[:, j_cols].bitcast(FP8X4),
+                    lhsT_scale=scales[:, j_cols],
+                    rhs=x_codes[:].bitcast(FP8X4),
+                    rhs_scale=x_scales[:],
+                    start=True,
+                    stop=True,
+                )
+            t_bank[z] = bank
+
+        def round_t(z):
+            g = z // GROUP
+            if z % GROUP == 0:
+                t_grouped[g] = t_pool.tile([P, GROUP, P, PACK], BF16, name="t_grouped", align_bytes=64)
+            nc.scalar.copy(out=t_grouped[g][:, z % GROUP], in_=t_bank[z][:].rearrange("p b x -> p x b"))
+
+        def second_product(g):
+            codes = t_pool.tile([P, GROUP * P], U32, name="t_codes", align_bytes=64)
+            scales = t_pool.tile([P, GROUP * P], U8, name="t_scales", align_bytes=64)
+            nc.vector.quantize_mx(
+                out=codes[:].bitcast(FP8X4),
+                scales=scales[:],
+                in_=t_grouped[g][:].rearrange("p m x b -> p (m x b)"),
+            )
+            bank = psum_out.tile([P, GROUP, P], F32, name="out_bank")
+            for m in range(GROUP):
+                x_cols = slice(m * P, (m + 1) * P)
+                nc.tensor.matmul_mx(
+                    out=bank[:, m, :],
+                    lhsT=codes[:, x_cols].bitcast(FP8X4),
+                    lhsT_scale=scales[:, x_cols],
+                    rhs=y_codes[:].bitcast(FP8X4),
+                    rhs_scale=y_scales[:],
+                    start=True,
+                    stop=True,
+                )
+            out_bank[g] = bank
+
+        def gather(g, ys):
+            nc.scalar.copy(
+                out=out_sb[:, ys, g * GROUP : (g + 1) * GROUP],
+                in_=out_bank[g][:, :, ys].rearrange("p m y -> p y m"),
+            )
+
+        def maps_at(z):
+            return [z] if 0 <= z < N_MAPS else []
+
+        def groups_ending_at(z):
+            return [z // GROUP] if 0 <= z < N_MAPS and z % GROUP == GROUP - 1 else []
+
+        regroup(0)
+        x_codes, x_scales = transpose_and_quantise(
+            nc, psum_t, keep, x1[:].rearrange("n (p t) -> n t p", t=PACK), ident, "x"
+        )
+        y1_sorted = keep.tile([P, PACK, P], BF16, name="y1_sorted")
+        nc.vector.tensor_copy(
+            out=y1_sorted[:].rearrange("n b (q r) -> n q b r", r=RUN),
+            in_=y1[:].rearrange("n (q b r) -> n q b r", b=PACK, r=RUN),
+        )
+        y_codes, y_scales = transpose_and_quantise(nc, psum_t, keep, y1_sorted[:], ident, "y")
+        for step in range(N_MAPS + SECOND_LAG):
+            for z in maps_at(step + 1):
+                regroup(z)
+            for z in maps_at(step):
+                first_product(z)
+            for z in maps_at(step - ROUND_LAG):
+                round_t(z)
+            for g in groups_ending_at(step - SECOND_LAG):
+                second_product(g)
+            for g in groups_ending_at(step - GATHER_LAG):
+                gather(g, slice(0, P))
+
+        y_chunk = P // STORE_CHUNKS
+        for c in range(STORE_CHUNKS):
+            ys = slice(c * y_chunk, (c + 1) * y_chunk)
+            gather(N_GROUPS - 1, ys)
+            nc.sync.dma_start(out=out_rows[:, ys, :], in_=out_sb[:, ys, :])

@@ -26,13 +26,15 @@ ROUND_LAG = 2
 SECOND_LAG = 15
 GATHER_LAG = 17
 
+Y_STEP = 6
+
 STORE_CHUNKS = 4
 
 
 def load_with_ones(nc, pool, feats, name):
     full = pool.tile([P, K], BF16, name=name)
     nc.vector.memset(full[:, K - 16 : K], 1.0)
-    nc.scalar.dma_start(out=full[:, 0 : K - 1], in_=feats.rearrange("b n f -> (b n) f"))
+    nc.sync.dma_start(out=full[:, 0 : K - 1], in_=feats.rearrange("b n f -> (b n) f"))
     return full
 
 
@@ -67,8 +69,10 @@ def tile_span2oscorer_pa_kernel(tc, xp, yp, w, out):
             raw_z = raw_pool.tile([P, PACK, K], BF16, name="raw_z")
             nc.sync.dma_start(out=raw_z[:], in_=w[0, z].rearrange("(p t) j -> p t j", t=PACK))
             raw.append(raw_z)
-        x1 = load_with_ones(nc, keep, xp, "x1")
-        y1 = load_with_ones(nc, keep, yp, "y1")
+            if z == 0:
+                x1 = load_with_ones(nc, keep, xp, "x1")
+            if z == Y_STEP:
+                y1 = load_with_ones(nc, keep, yp, "y1")
 
         ident = keep.tile([P, P], BF16, name="ident")
         masks.make_identity(nc, ident[:])
@@ -154,12 +158,6 @@ def tile_span2oscorer_pa_kernel(tc, xp, yp, w, out):
         x_codes, x_scales = transpose_and_quantise(
             nc, psum_t, keep, x1[:].rearrange("n (p t) -> n t p", t=PACK), ident, "x"
         )
-        y1_sorted = keep.tile([P, PACK, P], BF16, name="y1_sorted")
-        nc.vector.tensor_copy(
-            out=y1_sorted[:].rearrange("n b (q r) -> n q b r", r=RUN),
-            in_=y1[:].rearrange("n (q b r) -> n q b r", b=PACK, r=RUN),
-        )
-        y_codes, y_scales = transpose_and_quantise(nc, psum_t, keep, y1_sorted[:], ident, "y")
         for step in range(N_MAPS + SECOND_LAG):
             for z in maps_at(step + 1):
                 regroup(z)
@@ -167,6 +165,13 @@ def tile_span2oscorer_pa_kernel(tc, xp, yp, w, out):
                 first_product(z)
             for z in maps_at(step - ROUND_LAG):
                 round_t(z)
+            if step == Y_STEP:
+                y1_sorted = keep.tile([P, PACK, P], BF16, name="y1_sorted")
+                nc.vector.tensor_copy(
+                    out=y1_sorted[:].rearrange("n b (q r) -> n q b r", r=RUN),
+                    in_=y1[:].rearrange("n (q b r) -> n q b r", b=PACK, r=RUN),
+                )
+                y_codes, y_scales = transpose_and_quantise(nc, psum_t, keep, y1_sorted[:], ident, "y")
             for g in groups_ending_at(step - SECOND_LAG):
                 second_product(g)
             for g in groups_ending_at(step - GATHER_LAG):

@@ -21,6 +21,8 @@ FLOPS = 2 * N_MAPS * P * K * K + 2 * N_MAPS * P * P * K
 RUN = 8
 N_BLOCKS = K // (PACK * RUN)
 VECTOR_BLOCKS = 10
+PASS_STEP = 4
+PASS_BS = (2, 3)
 
 ROUND_LAG = 2
 SECOND_LAG = 15
@@ -61,8 +63,9 @@ def tile_span2oscorer_pa_kernel(tc, xp, yp, w, out):
         raw_pool = ctx.enter_context(tc.tile_pool(name="raw", bufs=N_MAPS))
         map_pool = ctx.enter_context(tc.tile_pool(name="map", bufs=4))
         t_pool = ctx.enter_context(tc.tile_pool(name="t", bufs=6))
-        psum_t = ctx.enter_context(tc.psum_pool(name="psum_t", bufs=4))
-        psum_out = ctx.enter_context(tc.psum_pool(name="psum_out", bufs=4))
+        psum_t = ctx.enter_context(tc.psum_pool(name="psum_t", bufs=3))
+        psum_out = ctx.enter_context(tc.psum_pool(name="psum_out", bufs=3))
+        psum_pass = ctx.enter_context(tc.psum_pool(name="psum_pass", bufs=2))
 
         raw = []
         for z in range(N_MAPS):
@@ -79,17 +82,35 @@ def tile_span2oscorer_pa_kernel(tc, xp, yp, w, out):
         out_sb = keep.tile([P, P, N_MAPS], F32, name="out_sb")
         out_rows = out.rearrange("b x y z -> (b x) y z")
 
+        passed = {}
         map_grouped = {}
         t_bank = {}
         t_grouped = {}
         out_bank = {}
 
+        def is_passed(z):
+            return z % PASS_STEP == 2
+
+        def pass_through(z):
+            bank = psum_pass.tile([P, len(PASS_BS), K], BF16, name="pass_bank")
+            src = raw[z][:].rearrange("p t (q b r) -> p b q r t", b=PACK, r=RUN)
+            for n, b in enumerate(PASS_BS):
+                nc.tensor.matmul(out=bank[:, n, :], lhsT=ident[:], rhs=src[:, b], start=True, stop=True)
+            passed[z] = bank
+
         def regroup(z):
             grouped = map_pool.tile([P, K, PACK], BF16, name="map_grouped", align_bytes=64)
             src = raw[z][:].rearrange("p t (q b r) -> p q b t r", b=PACK, r=RUN)
             dst = grouped[:].rearrange("p (b q r) t -> p q b t r", b=PACK, r=RUN)
-            nc.vector.tensor_copy(out=dst[:, :VECTOR_BLOCKS], in_=src[:, :VECTOR_BLOCKS])
-            nc.scalar.copy(out=dst[:, VECTOR_BLOCKS:], in_=src[:, VECTOR_BLOCKS:])
+            if is_passed(z):
+                nc.vector.tensor_copy(out=dst[:, :, : PASS_BS[0]], in_=src[:, :, : PASS_BS[0]])
+                nc.scalar.copy(
+                    out=grouped[:, PASS_BS[0] * P :, :].rearrange("p c t -> p (c t)"),
+                    in_=passed[z][:].rearrange("p b c -> p (b c)"),
+                )
+            else:
+                nc.vector.tensor_copy(out=dst[:, :VECTOR_BLOCKS], in_=src[:, :VECTOR_BLOCKS])
+                nc.scalar.copy(out=dst[:, VECTOR_BLOCKS:], in_=src[:, VECTOR_BLOCKS:])
             map_grouped[z] = grouped
 
         def first_product(z):
@@ -159,6 +180,9 @@ def tile_span2oscorer_pa_kernel(tc, xp, yp, w, out):
             nc, psum_t, keep, x1[:].rearrange("n (p t) -> n t p", t=PACK), ident, "x"
         )
         for step in range(N_MAPS + SECOND_LAG):
+            for z in maps_at(step + 2):
+                if is_passed(z):
+                    pass_through(z)
             for z in maps_at(step + 1):
                 regroup(z)
             for z in maps_at(step):

@@ -93,9 +93,10 @@ def tile_span2oscorer_pa_kernel(tc, xp, yp, w, out):
 
         def pass_through(z):
             bank = psum_pass.tile([P, len(PASS_BS), K], BF16, name="pass_bank")
-            src = raw[z][:].rearrange("p t (q b r) -> p b q r t", b=PACK, r=RUN)
+            src = raw[z][:].rearrange("p t (q b r) -> p b t q r", b=PACK, r=RUN)
+            dst = bank[:].rearrange("p n (q r t) -> p n t q r", r=RUN, t=PACK)
             for n, b in enumerate(PASS_BS):
-                nc.tensor.matmul(out=bank[:, n, :], lhsT=ident[:], rhs=src[:, b], start=True, stop=True)
+                nc.tensor.matmul(out=dst[:, n], lhsT=ident[:], rhs=src[:, b], start=True, stop=True)
             passed[z] = bank
 
         def regroup(z):

@@ -24,10 +24,11 @@ VECTOR_BLOCKS = 10
 PASS_STEP = 4
 PASS_BS = (2, 3)
 
-ROUND_LAG = 2
-SECOND_LAG = 15
-GATHER_LAG = 17
+ROUND_LAG = 1
+SECOND_LAG = 12
+GATHER_LAG = 15
 
+Y_LOAD = 3
 Y_STEP = 6
 
 STORE_CHUNKS = 4
@@ -40,12 +41,16 @@ def load_with_ones(nc, pool, feats, name):
     return full
 
 
-def transpose_and_quantise(nc, psum, pool, planes, ident, name):
+def transpose_and_group(nc, psum, pool, planes, ident, name):
     turned = psum.tile([P, PACK, P], BF16, name="turned", tag="t_bank")
     for t in range(PACK):
         nc.tensor.transpose(turned[:, t, :], planes[:, t, :], ident[:])
     grouped = pool.tile([P, P, PACK], BF16, name=name + "_grouped", align_bytes=64)
     nc.scalar.copy(out=grouped[:], in_=turned[:].rearrange("p t n -> p n t"))
+    return grouped
+
+
+def quantise_features(nc, pool, grouped, name):
     codes = pool.tile([P, P], U32, name=name + "_codes", align_bytes=64)
     scales = pool.tile([P, P], U8, name=name + "_scales", align_bytes=64)
     nc.vector.quantize_mx(
@@ -61,7 +66,7 @@ def tile_span2oscorer_pa_kernel(tc, xp, yp, w, out):
     with ExitStack() as ctx:
         keep = ctx.enter_context(tc.tile_pool(name="keep", bufs=1))
         raw_pool = ctx.enter_context(tc.tile_pool(name="raw", bufs=N_MAPS))
-        map_pool = ctx.enter_context(tc.tile_pool(name="map", bufs=4))
+        map_pool = ctx.enter_context(tc.tile_pool(name="map", bufs=5))
         t_pool = ctx.enter_context(tc.tile_pool(name="t", bufs=6))
         psum_t = ctx.enter_context(tc.psum_pool(name="psum_t", bufs=3))
         psum_out = ctx.enter_context(tc.psum_pool(name="psum_out", bufs=3))
@@ -74,7 +79,7 @@ def tile_span2oscorer_pa_kernel(tc, xp, yp, w, out):
             raw.append(raw_z)
             if z == 0:
                 x1 = load_with_ones(nc, keep, xp, "x1")
-            if z == Y_STEP:
+            if z == Y_LOAD:
                 y1 = load_with_ones(nc, keep, yp, "y1")
 
         ident = keep.tile([P, P], BF16, name="ident")
@@ -176,8 +181,13 @@ def tile_span2oscorer_pa_kernel(tc, xp, yp, w, out):
         def groups_ending_at(z):
             return [z // GROUP] if 0 <= z < N_MAPS and z % GROUP == GROUP - 1 else []
 
+        ctx.enter_context(
+            tc.manual_schedule(
+                engines={mybir.EngineType.DVE, mybir.EngineType.Activation, mybir.EngineType.PE}
+            )
+        )
         regroup(0)
-        x_codes, x_scales = transpose_and_quantise(
+        x_grouped = transpose_and_group(
             nc, psum_t, keep, x1[:].rearrange("n (p t) -> n t p", t=PACK), ident, "x"
         )
         for step in range(N_MAPS + SECOND_LAG):
@@ -186,6 +196,8 @@ def tile_span2oscorer_pa_kernel(tc, xp, yp, w, out):
                     pass_through(z)
             for z in maps_at(step + 1):
                 regroup(z)
+            if step == 0:
+                x_codes, x_scales = quantise_features(nc, keep, x_grouped, "x")
             for z in maps_at(step):
                 first_product(z)
             for z in maps_at(step - ROUND_LAG):
@@ -196,7 +208,10 @@ def tile_span2oscorer_pa_kernel(tc, xp, yp, w, out):
                     out=y1_sorted[:].rearrange("n b (q r) -> n q b r", r=RUN),
                     in_=y1[:].rearrange("n (q b r) -> n q b r", b=PACK, r=RUN),
                 )
-                y_codes, y_scales = transpose_and_quantise(nc, psum_t, keep, y1_sorted[:], ident, "y")
+            if step == Y_STEP + 1:
+                y_grouped = transpose_and_group(nc, psum_t, keep, y1_sorted[:], ident, "y")
+            if step == Y_STEP + 2:
+                y_codes, y_scales = quantise_features(nc, keep, y_grouped, "y")
             for g in groups_ending_at(step - SECOND_LAG):
                 second_product(g)
             for g in groups_ending_at(step - GATHER_LAG):

@@ -21,12 +21,13 @@ FLOPS = 2 * N_MAPS * P * K * K + 2 * N_MAPS * P * P * K
 RUN = 8
 N_BLOCKS = K // (PACK * RUN)
 VECTOR_BLOCKS = 10
-PASS_STEP = 4
-PASS_BS = (2, 3)
+PASS_BLOCKS = 2
+PASS_COLS = PASS_BLOCKS * PACK * RUN
 
 ROUND_LAG = 1
-SECOND_LAG = 12
-GATHER_LAG = 15
+SECOND_LAG = 11
+GATHER_LAG = 12
+LATE_GROUP = 5
 
 Y_LOAD = 3
 Y_STEP = 6
@@ -41,10 +42,14 @@ def load_with_ones(nc, pool, feats, name):
     return full
 
 
-def transpose_and_group(nc, psum, pool, planes, ident, name):
+def transpose_features(nc, psum, planes, ident):
     turned = psum.tile([P, PACK, P], BF16, name="turned", tag="t_bank")
     for t in range(PACK):
         nc.tensor.transpose(turned[:, t, :], planes[:, t, :], ident[:])
+    return turned
+
+
+def group_features(nc, pool, turned, name):
     grouped = pool.tile([P, P, PACK], BF16, name=name + "_grouped", align_bytes=64)
     nc.scalar.copy(out=grouped[:], in_=turned[:].rearrange("p t n -> p n t"))
     return grouped
@@ -89,37 +94,38 @@ def tile_span2oscorer_pa_kernel(tc, xp, yp, w, out):
 
         passed = {}
         map_grouped = {}
+        map_codes = {}
+        map_scales = {}
         t_bank = {}
         t_grouped = {}
+        t_codes = {}
+        t_scales = {}
         out_bank = {}
 
-        def is_passed(z):
-            return z % PASS_STEP == 2
-
         def pass_through(z):
-            bank = psum_pass.tile([P, len(PASS_BS), K], BF16, name="pass_bank")
-            src = raw[z][:].rearrange("p t (q b r) -> p b t q r", b=PACK, r=RUN)
-            dst = bank[:].rearrange("p n (q r t) -> p n t q r", r=RUN, t=PACK)
-            for n, b in enumerate(PASS_BS):
-                nc.tensor.matmul(out=dst[:, n], lhsT=ident[:], rhs=src[:, b], start=True, stop=True)
+            bank = psum_pass.tile([P, PASS_COLS, PACK], BF16, name="pass_bank")
+            nc.tensor.matmul(
+                out=bank[:].rearrange("p j t -> p t j"),
+                lhsT=ident[:],
+                rhs=raw[z][:, :, K - PASS_COLS :],
+                start=True,
+                stop=True,
+            )
             passed[z] = bank
 
         def regroup(z):
             grouped = map_pool.tile([P, K, PACK], BF16, name="map_grouped", align_bytes=64)
             src = raw[z][:].rearrange("p t (q b r) -> p q b t r", b=PACK, r=RUN)
             dst = grouped[:].rearrange("p (b q r) t -> p q b t r", b=PACK, r=RUN)
-            if is_passed(z):
-                nc.vector.tensor_copy(out=dst[:, :, : PASS_BS[0]], in_=src[:, :, : PASS_BS[0]])
-                nc.scalar.copy(
-                    out=grouped[:, PASS_BS[0] * P :, :].rearrange("p c t -> p (c t)"),
-                    in_=passed[z][:].rearrange("p b c -> p (b c)"),
-                )
-            else:
-                nc.vector.tensor_copy(out=dst[:, :VECTOR_BLOCKS], in_=src[:, :VECTOR_BLOCKS])
-                nc.scalar.copy(out=dst[:, VECTOR_BLOCKS:], in_=src[:, VECTOR_BLOCKS:])
+            nc.vector.tensor_copy(out=dst[:, :VECTOR_BLOCKS], in_=src[:, :VECTOR_BLOCKS])
+            nc.scalar.copy(out=dst[:, VECTOR_BLOCKS:-PASS_BLOCKS], in_=src[:, VECTOR_BLOCKS:-PASS_BLOCKS])
+            nc.scalar.copy(
+                out=grouped[:].rearrange("p (b q r) t -> p q b (r t)", b=PACK, r=RUN)[:, -PASS_BLOCKS:],
+                in_=passed[z][:].rearrange("p (q b r) t -> p q b (r t)", b=PACK, r=RUN),
+            )
             map_grouped[z] = grouped
 
-        def first_product(z):
+        def quantise_map(z):
             codes = map_pool.tile([P, K], U32, name="map_codes", align_bytes=64)
             scales = map_pool.tile([P, K], U8, name="map_scales", align_bytes=64)
             nc.vector.quantize_mx(
@@ -127,13 +133,17 @@ def tile_span2oscorer_pa_kernel(tc, xp, yp, w, out):
                 scales=scales[:],
                 in_=map_grouped[z][:].rearrange("p j t -> p (j t)"),
             )
+            map_codes[z] = codes
+            map_scales[z] = scales
+
+        def first_product(z):
             bank = psum_t.tile([P, PACK, P], F32, name="t_bank")
             for b in range(PACK):
                 j_cols = slice(b * P, (b + 1) * P)
                 nc.tensor.matmul_mx(
                     out=bank[:, b, :],
-                    lhsT=codes[:, j_cols].bitcast(FP8X4),
-                    lhsT_scale=scales[:, j_cols],
+                    lhsT=map_codes[z][:, j_cols].bitcast(FP8X4),
+                    lhsT_scale=map_scales[z][:, j_cols],
                     rhs=x_codes[:].bitcast(FP8X4),
                     rhs_scale=x_scales[:],
                     start=True,
@@ -147,30 +157,31 @@ def tile_span2oscorer_pa_kernel(tc, xp, yp, w, out):
                 t_grouped[g] = t_pool.tile([P, GROUP, P, PACK], BF16, name="t_grouped", align_bytes=64)
             nc.scalar.copy(out=t_grouped[g][:, z % GROUP], in_=t_bank[z][:].rearrange("p b x -> p x b"))
 
-        def second_product(g):
-            codes = t_pool.tile([P, GROUP * P], U32, name="t_codes", align_bytes=64)
-            scales = t_pool.tile([P, GROUP * P], U8, name="t_scales", align_bytes=64)
+        def second_product(g, first, count):
+            if first == 0:
+                t_codes[g] = t_pool.tile([P, GROUP * P], U32, name="t_codes", align_bytes=64)
+                t_scales[g] = t_pool.tile([P, GROUP * P], U8, name="t_scales", align_bytes=64)
+                out_bank[g] = psum_out.tile([P, GROUP, P], F32, name="out_bank")
+            cols = slice(first * P, (first + count) * P)
             nc.vector.quantize_mx(
-                out=codes[:].bitcast(FP8X4),
-                scales=scales[:],
-                in_=t_grouped[g][:].rearrange("p m x b -> p (m x b)"),
+                out=t_codes[g][:, cols].bitcast(FP8X4),
+                scales=t_scales[g][:, cols],
+                in_=t_grouped[g][:, first : first + count].rearrange("p m x b -> p (m x b)"),
             )
-            bank = psum_out.tile([P, GROUP, P], F32, name="out_bank")
-            for m in range(GROUP):
+            for m in range(first, first + count):
                 x_cols = slice(m * P, (m + 1) * P)
                 nc.tensor.matmul_mx(
-                    out=bank[:, m, :],
-                    lhsT=codes[:, x_cols].bitcast(FP8X4),
-                    lhsT_scale=scales[:, x_cols],
+                    out=out_bank[g][:, m, :],
+                    lhsT=t_codes[g][:, x_cols].bitcast(FP8X4),
+                    lhsT_scale=t_scales[g][:, x_cols],
                     rhs=y_codes[:].bitcast(FP8X4),
                     rhs_scale=y_scales[:],
                     start=True,
                     stop=True,
                 )
-            out_bank[g] = bank
 
-        def gather(g, ys):
-            nc.scalar.copy(
+        def gather(copy, g, ys):
+            copy(
                 out=out_sb[:, ys, g * GROUP : (g + 1) * GROUP],
                 in_=out_bank[g][:, :, ys].rearrange("p m y -> p y m"),
             )
@@ -179,26 +190,29 @@ def tile_span2oscorer_pa_kernel(tc, xp, yp, w, out):
             return [z] if 0 <= z < N_MAPS else []
 
         def groups_ending_at(z):
-            return [z // GROUP] if 0 <= z < N_MAPS and z % GROUP == GROUP - 1 else []
+            return [z // GROUP] if 0 <= z < LATE_GROUP * GROUP and z % GROUP == GROUP - 1 else []
 
         ctx.enter_context(
             tc.manual_schedule(
                 engines={mybir.EngineType.DVE, mybir.EngineType.Activation, mybir.EngineType.PE}
             )
         )
+        pass_through(0)
         regroup(0)
-        x_grouped = transpose_and_group(
-            nc, psum_t, keep, x1[:].rearrange("n (p t) -> n t p", t=PACK), ident, "x"
-        )
-        for step in range(N_MAPS + SECOND_LAG):
+        quantise_map(0)
+        x_turned = transpose_features(nc, psum_t, x1[:].rearrange("n (p t) -> n t p", t=PACK), ident)
+        x_grouped = group_features(nc, keep, x_turned, "x")
+        pass_through(1)
+        for step in range(N_MAPS + ROUND_LAG):
             for z in maps_at(step + 2):
-                if is_passed(z):
-                    pass_through(z)
+                pass_through(z)
             for z in maps_at(step + 1):
                 regroup(z)
             if step == 0:
                 x_codes, x_scales = quantise_features(nc, keep, x_grouped, "x")
             for z in maps_at(step):
+                if z > 0:
+                    quantise_map(z)
                 first_product(z)
             for z in maps_at(step - ROUND_LAG):
                 round_t(z)
@@ -209,16 +223,27 @@ def tile_span2oscorer_pa_kernel(tc, xp, yp, w, out):
                     in_=y1[:].rearrange("n (q b r) -> n q b r", b=PACK, r=RUN),
                 )
             if step == Y_STEP + 1:
-                y_grouped = transpose_and_group(nc, psum_t, keep, y1_sorted[:], ident, "y")
+                y_turned = transpose_features(nc, psum_t, y1_sorted[:], ident)
             if step == Y_STEP + 2:
+                y_grouped = group_features(nc, keep, y_turned, "y")
+            if step == Y_STEP + 3:
                 y_codes, y_scales = quantise_features(nc, keep, y_grouped, "y")
             for g in groups_ending_at(step - SECOND_LAG):
-                second_product(g)
+                second_product(g, 0, GROUP)
             for g in groups_ending_at(step - GATHER_LAG):
-                gather(g, slice(0, P))
+                gather(nc.scalar.copy, g, slice(0, P))
+
+        last = N_GROUPS - 1
+        second_product(last, 0, 2)
+        for g in range(LATE_GROUP, last):
+            second_product(g, 0, GROUP)
+        second_product(last, 2, 1)
+        second_product(last, 3, 1)
+        gather(nc.scalar.copy, last - 2, slice(0, P))
+        gather(nc.vector.tensor_copy, last - 1, slice(0, P))
 
         y_chunk = P // STORE_CHUNKS
         for c in range(STORE_CHUNKS):
             ys = slice(c * y_chunk, (c + 1) * y_chunk)
-            gather(N_GROUPS - 1, ys)
+            gather(nc.scalar.copy, last, ys)
             nc.sync.dma_start(out=out_rows[:, ys, :], in_=out_sb[:, ys, :])

@@ -20,7 +20,10 @@ FLOPS = 2 * N_MAPS * P * K * K + 2 * N_MAPS * P * P * K
 
 RUN = 8
 N_BLOCKS = K // (PACK * RUN)
-VECTOR_BLOCKS = 10
+def vector_blocks(z):
+    return 8 if z % 4 == 1 else 10
+
+
 PASS_BLOCKS = 2
 PASS_COLS = PASS_BLOCKS * PACK * RUN
 
@@ -117,8 +120,9 @@ def tile_span2oscorer_pa_kernel(tc, xp, yp, w, out):
             grouped = map_pool.tile([P, K, PACK], BF16, name="map_grouped", align_bytes=64)
             src = raw[z][:].rearrange("p t (q b r) -> p q b t r", b=PACK, r=RUN)
             dst = grouped[:].rearrange("p (b q r) t -> p q b t r", b=PACK, r=RUN)
-            nc.vector.tensor_copy(out=dst[:, :VECTOR_BLOCKS], in_=src[:, :VECTOR_BLOCKS])
-            nc.scalar.copy(out=dst[:, VECTOR_BLOCKS:-PASS_BLOCKS], in_=src[:, VECTOR_BLOCKS:-PASS_BLOCKS])
+            cut = vector_blocks(z)
+            nc.vector.tensor_copy(out=dst[:, :cut], in_=src[:, :cut])
+            nc.scalar.copy(out=dst[:, cut:-PASS_BLOCKS], in_=src[:, cut:-PASS_BLOCKS])
             nc.scalar.copy(
                 out=grouped[:].rearrange("p (b q r) t -> p q b (r t)", b=PACK, r=RUN)[:, -PASS_BLOCKS:],
                 in_=passed[z][:].rearrange("p (q b r) t -> p q b (r t)", b=PACK, r=RUN),

@@ -21,7 +21,7 @@ FLOPS = 2 * N_MAPS * P * K * K + 2 * N_MAPS * P * P * K
 RUN = 8
 N_BLOCKS = K // (PACK * RUN)
 def vector_blocks(z):
-    return 8 if z % 4 == 1 else 10
+    return 8 if z % 5 == 1 and z < N_MAPS - GROUP else 10
 
 
 PASS_BLOCKS = 2
@@ -238,11 +238,10 @@ def tile_span2oscorer_pa_kernel(tc, xp, yp, w, out):
                 gather(nc.scalar.copy, g, slice(0, P))
 
         last = N_GROUPS - 1
-        second_product(last, 0, 2)
         for g in range(LATE_GROUP, last):
             second_product(g, 0, GROUP)
-        second_product(last, 2, 1)
-        second_product(last, 3, 1)
+        second_product(last, 0, GROUP // 2)
+        second_product(last, GROUP // 2, GROUP // 2)
         gather(nc.scalar.copy, last - 2, slice(0, P))
         gather(nc.vector.tensor_copy, last - 1, slice(0, P))
 

@@ -21,16 +21,17 @@ FLOPS = 2 * N_MAPS * P * K * K + 2 * N_MAPS * P * P * K
 RUN = 8
 N_BLOCKS = K // (PACK * RUN)
 def vector_blocks(z):
-    return 8 if z % 5 == 1 and z < N_MAPS - GROUP else 10
+    return 8 if z % 6 == 1 else 10
 
 
 PASS_BLOCKS = 2
 PASS_COLS = PASS_BLOCKS * PACK * RUN
 
-ROUND_LAG = 1
+ROUND_LAG = 2
 SECOND_LAG = 11
 GATHER_LAG = 12
 LATE_GROUP = 5
+LATE_GATHER = 4
 
 Y_LOAD = 3
 Y_STEP = 6
@@ -50,6 +51,23 @@ def transpose_features(nc, psum, planes, ident):
     for t in range(PACK):
         nc.tensor.transpose(turned[:, t, :], planes[:, t, :], ident[:])
     return turned
+
+
+def transpose_words(nc, psum, words, ident):
+    turned = psum.tile([P, 2, P], F32, name="turned_words", tag="t_bank")
+    for u in range(2):
+        nc.tensor.transpose(turned[:, u, :], words[:, u::2], ident[:])
+    return turned
+
+
+def group_words(nc, pool, turned, name):
+    grouped = pool.tile([P, P, PACK], BF16, name=name + "_grouped", align_bytes=64)
+    words = grouped[:].rearrange("p n t -> p (n t)").bitcast(F32)
+    nc.scalar.copy(
+        out=words.rearrange("p (n u) -> p n u", u=2),
+        in_=turned[:].rearrange("p u n -> p n u"),
+    )
+    return grouped
 
 
 def group_features(nc, pool, turned, name):
@@ -92,6 +110,8 @@ def tile_span2oscorer_pa_kernel(tc, xp, yp, w, out):
 
         ident = keep.tile([P, P], BF16, name="ident")
         masks.make_identity(nc, ident[:])
+        word_ident = keep.tile([P, P], F32, name="word_ident")
+        masks.make_identity(nc, word_ident[:])
         out_sb = keep.tile([P, P, N_MAPS], F32, name="out_sb")
         out_rows = out.rearrange("b x y z -> (b x) y z")
 
@@ -165,7 +185,10 @@ def tile_span2oscorer_pa_kernel(tc, xp, yp, w, out):
             if first == 0:
                 t_codes[g] = t_pool.tile([P, GROUP * P], U32, name="t_codes", align_bytes=64)
                 t_scales[g] = t_pool.tile([P, GROUP * P], U8, name="t_scales", align_bytes=64)
-                out_bank[g] = psum_out.tile([P, GROUP, P], F32, name="out_bank")
+                if g == N_GROUPS - 1:
+                    out_bank[g] = psum_t.tile([P, GROUP, P], F32, name="last_out_bank", tag="t_bank")
+                else:
+                    out_bank[g] = psum_out.tile([P, GROUP, P], F32, name="out_bank")
             cols = slice(first * P, (first + count) * P)
             nc.vector.quantize_mx(
                 out=t_codes[g][:, cols].bitcast(FP8X4),
@@ -204,8 +227,8 @@ def tile_span2oscorer_pa_kernel(tc, xp, yp, w, out):
         pass_through(0)
         regroup(0)
         quantise_map(0)
-        x_turned = transpose_features(nc, psum_t, x1[:].rearrange("n (p t) -> n t p", t=PACK), ident)
-        x_grouped = group_features(nc, keep, x_turned, "x")
+        x_turned = transpose_words(nc, psum_t, x1[:].bitcast(F32), word_ident)
+        x_grouped = group_words(nc, keep, x_turned, "x")
         pass_through(1)
         for step in range(N_MAPS + ROUND_LAG):
             for z in maps_at(step + 2):
@@ -222,7 +245,7 @@ def tile_span2oscorer_pa_kernel(tc, xp, yp, w, out):
                 round_t(z)
             if step == Y_STEP:
                 y1_sorted = keep.tile([P, PACK, P], BF16, name="y1_sorted")
-                nc.vector.tensor_copy(
+                nc.scalar.copy(
                     out=y1_sorted[:].rearrange("n b (q r) -> n q b r", r=RUN),
                     in_=y1[:].rearrange("n (q b r) -> n q b r", b=PACK, r=RUN),
                 )
@@ -235,18 +258,18 @@ def tile_span2oscorer_pa_kernel(tc, xp, yp, w, out):
             for g in groups_ending_at(step - SECOND_LAG):
                 second_product(g, 0, GROUP)
             for g in groups_ending_at(step - GATHER_LAG):
-                gather(nc.scalar.copy, g, slice(0, P))
+                if g < LATE_GATHER:
+                    gather(nc.scalar.copy, g, slice(0, P))
 
         last = N_GROUPS - 1
         for g in range(LATE_GROUP, last):
             second_product(g, 0, GROUP)
         second_product(last, 0, GROUP // 2)
         second_product(last, GROUP // 2, GROUP // 2)
-        gather(nc.scalar.copy, last - 2, slice(0, P))
-        gather(nc.vector.tensor_copy, last - 1, slice(0, P))
 
         y_chunk = P // STORE_CHUNKS
         for c in range(STORE_CHUNKS):
             ys = slice(c * y_chunk, (c + 1) * y_chunk)
-            gather(nc.scalar.copy, last, ys)
+            for g in range(LATE_GATHER, N_GROUPS):
+                gather(nc.scalar.copy if g in (LATE_GATHER, last) else nc.vector.tensor_copy, g, ys)
             nc.sync.dma_start(out=out_rows[:, ys, :], in_=out_sb[:, ys, :])

from contextlib import ExitStack

import concourse.masks as masks
import concourse.mybir as mybir

BF16 = mybir.dt.bfloat16
F32 = mybir.dt.float32
U32 = mybir.dt.uint32
U8 = mybir.dt.uint8
FP8X4 = mybir.dt.float8_e4m3fn_x4

P = 128
PACK = 4
K = P * PACK
N_MAPS = 32
GROUP = 4
N_GROUPS = N_MAPS // GROUP

FLOPS = 2 * N_MAPS * P * K * K + 2 * N_MAPS * P * P * K

RUN = 8
N_BLOCKS = K // (PACK * RUN)
def vector_blocks(z):
    return 8 if z % 6 == 1 else 10


PASS_BLOCKS = 2
PASS_COLS = PASS_BLOCKS * PACK * RUN

ROUND_LAG = 2
SECOND_LAG = 11
GATHER_LAG = 12
LATE_GROUP = 5
LATE_GATHER = 4

Y_LOAD = 3
Y_STEP = 6

STORE_CHUNKS = 4


def load_with_ones(nc, pool, feats, name):
    full = pool.tile([P, K], BF16, name=name)
    nc.vector.memset(full[:, K - 16 : K], 1.0)
    nc.sync.dma_start(out=full[:, 0 : K - 1], in_=feats.rearrange("b n f -> (b n) f"))
    return full


def transpose_features(nc, psum, planes, ident):
    turned = psum.tile([P, PACK, P], BF16, name="turned", tag="t_bank")
    for t in range(PACK):
        nc.tensor.transpose(turned[:, t, :], planes[:, t, :], ident[:])
    return turned


def transpose_words(nc, psum, words, ident):
    turned = psum.tile([P, 2, P], F32, name="turned_words", tag="t_bank")
    for u in range(2):
        nc.tensor.transpose(turned[:, u, :], words[:, u::2], ident[:])
    return turned


def group_words(nc, pool, turned, name):
    grouped = pool.tile([P, P, PACK], BF16, name=name + "_grouped", align_bytes=64)
    words = grouped[:].rearrange("p n t -> p (n t)").bitcast(F32)
    nc.scalar.copy(
        out=words.rearrange("p (n u) -> p n u", u=2),
        in_=turned[:].rearrange("p u n -> p n u"),
    )
    return grouped


def group_features(nc, pool, turned, name):
    grouped = pool.tile([P, P, PACK], BF16, name=name + "_grouped", align_bytes=64)
    nc.scalar.copy(out=grouped[:], in_=turned[:].rearrange("p t n -> p n t"))
    return grouped


def quantise_features(nc, pool, grouped, name):
    codes = pool.tile([P, P], U32, name=name + "_codes", align_bytes=64)
    scales = pool.tile([P, P], U8, name=name + "_scales", align_bytes=64)
    nc.vector.quantize_mx(
        out=codes[:].bitcast(FP8X4),
        scales=scales[:],
        in_=grouped[:].rearrange("p n t -> p (n t)"),
    )
    return codes, scales


def tile_span2oscorer_pa_kernel(tc, xp, yp, w, out):
    nc = tc.nc
    with ExitStack() as ctx:
        keep = ctx.enter_context(tc.tile_pool(name="keep", bufs=1))
        raw_pool = ctx.enter_context(tc.tile_pool(name="raw", bufs=N_MAPS))
        map_pool = ctx.enter_context(tc.tile_pool(name="map", bufs=5))
        t_pool = ctx.enter_context(tc.tile_pool(name="t", bufs=6))
        psum_t = ctx.enter_context(tc.psum_pool(name="psum_t", bufs=3))
        psum_out = ctx.enter_context(tc.psum_pool(name="psum_out", bufs=3))
        psum_pass = ctx.enter_context(tc.psum_pool(name="psum_pass", bufs=2))

        raw = []
        for z in range(N_MAPS):
            raw_z = raw_pool.tile([P, PACK, K], BF16, name="raw_z")
            nc.sync.dma_start(out=raw_z[:], in_=w[0, z].rearrange("(p t) j -> p t j", t=PACK))
            raw.append(raw_z)
            if z == 0:
                x1 = load_with_ones(nc, keep, xp, "x1")
            if z == Y_LOAD:
                y1 = load_with_ones(nc, keep, yp, "y1")

        ident = keep.tile([P, P], BF16, name="ident")
        masks.make_identity(nc, ident[:])
        word_ident = keep.tile([P, P], F32, name="word_ident")
        masks.make_identity(nc, word_ident[:])
        out_sb = keep.tile([P, P, N_MAPS], F32, name="out_sb")
        out_rows = out.rearrange("b x y z -> (b x) y z")

        passed = {}
        map_grouped = {}
        map_codes = {}
        map_scales = {}
        t_bank = {}
        t_grouped = {}
        t_codes = {}
        t_scales = {}
        out_bank = {}

        def pass_through(z):
            bank = psum_pass.tile([P, PASS_COLS, PACK], BF16, name="pass_bank")
            nc.tensor.matmul(
                out=bank[:].rearrange("p j t -> p t j"),
                lhsT=ident[:],
                rhs=raw[z][:, :, K - PASS_COLS :],
                start=True,
                stop=True,
            )
            passed[z] = bank

        def regroup(z):
            grouped = map_pool.tile([P, K, PACK], BF16, name="map_grouped", align_bytes=64)
            src = raw[z][:].rearrange("p t (q b r) -> p q b t r", b=PACK, r=RUN)
            dst = grouped[:].rearrange("p (b q r) t -> p q b t r", b=PACK, r=RUN)
            cut = vector_blocks(z)
            nc.vector.tensor_copy(out=dst[:, :cut], in_=src[:, :cut])
            nc.scalar.copy(out=dst[:, cut:-PASS_BLOCKS], in_=src[:, cut:-PASS_BLOCKS])
            nc.scalar.copy(
                out=grouped[:].rearrange("p (b q r) t -> p q b (r t)", b=PACK, r=RUN)[:, -PASS_BLOCKS:],
                in_=passed[z][:].rearrange("p (q b r) t -> p q b (r t)", b=PACK, r=RUN),
            )
            map_grouped[z] = grouped

        def quantise_map(z):
            codes = map_pool.tile([P, K], U32, name="map_codes", align_bytes=64)
            scales = map_pool.tile([P, K], U8, name="map_scales", align_bytes=64)
            nc.vector.quantize_mx(
                out=codes[:].bitcast(FP8X4),
                scales=scales[:],
                in_=map_grouped[z][:].rearrange("p j t -> p (j t)"),
            )
            map_codes[z] = codes
            map_scales[z] = scales

        def first_product(z):
            bank = psum_t.tile([P, PACK, P], F32, name="t_bank")
            for b in range(PACK):
                j_cols = slice(b * P, (b + 1) * P)
                nc.tensor.matmul_mx(
                    out=bank[:, b, :],
                    lhsT=map_codes[z][:, j_cols].bitcast(FP8X4),
                    lhsT_scale=map_scales[z][:, j_cols],
                    rhs=x_codes[:].bitcast(FP8X4),
                    rhs_scale=x_scales[:],
                    start=True,
                    stop=True,
                )
            t_bank[z] = bank

        def round_t(z):
            g = z // GROUP
            if z % GROUP == 0:
                t_grouped[g] = t_pool.tile([P, GROUP, P, PACK], BF16, name="t_grouped", align_bytes=64)
            nc.scalar.copy(out=t_grouped[g][:, z % GROUP], in_=t_bank[z][:].rearrange("p b x -> p x b"))

        def second_product(g, first, count):
            if first == 0:
                t_codes[g] = t_pool.tile([P, GROUP * P], U32, name="t_codes", align_bytes=64)
                t_scales[g] = t_pool.tile([P, GROUP * P], U8, name="t_scales", align_bytes=64)
                if g == N_GROUPS - 1:
                    out_bank[g] = psum_t.tile([P, GROUP, P], F32, name="last_out_bank", tag="t_bank")
                else:
                    out_bank[g] = psum_out.tile([P, GROUP, P], F32, name="out_bank")
            cols = slice(first * P, (first + count) * P)
            nc.vector.quantize_mx(
                out=t_codes[g][:, cols].bitcast(FP8X4),
                scales=t_scales[g][:, cols],
                in_=t_grouped[g][:, first : first + count].rearrange("p m x b -> p (m x b)"),
            )
            for m in range(first, first + count):
                x_cols = slice(m * P, (m + 1) * P)
                nc.tensor.matmul_mx(
                    out=out_bank[g][:, m, :],
                    lhsT=t_codes[g][:, x_cols].bitcast(FP8X4),
                    lhsT_scale=t_scales[g][:, x_cols],
                    rhs=y_codes[:].bitcast(FP8X4),
                    rhs_scale=y_scales[:],
                    start=True,
                    stop=True,
                )

        def gather(copy, g, ys):
            copy(
                out=out_sb[:, ys, g * GROUP : (g + 1) * GROUP],
                in_=out_bank[g][:, :, ys].rearrange("p m y -> p y m"),
            )

        def maps_at(z):
            return [z] if 0 <= z < N_MAPS else []

        def groups_ending_at(z):
            return [z // GROUP] if 0 <= z < LATE_GROUP * GROUP and z % GROUP == GROUP - 1 else []

        ctx.enter_context(
            tc.manual_schedule(
                engines={mybir.EngineType.DVE, mybir.EngineType.Activation, mybir.EngineType.PE}
            )
        )
        pass_through(0)
        regroup(0)
        quantise_map(0)
        x_turned = transpose_words(nc, psum_t, x1[:].bitcast(F32), word_ident)
        x_grouped = group_words(nc, keep, x_turned, "x")
        pass_through(1)
        for step in range(N_MAPS + ROUND_LAG):
            for z in maps_at(step + 2):
                pass_through(z)
            for z in maps_at(step + 1):
                regroup(z)
            if step == 0:
                x_codes, x_scales = quantise_features(nc, keep, x_grouped, "x")
            for z in maps_at(step):
                if z > 0:
                    quantise_map(z)
                first_product(z)
            for z in maps_at(step - ROUND_LAG):
                round_t(z)
            if step == Y_STEP:
                y1_sorted = keep.tile([P, PACK, P], BF16, name="y1_sorted")
                nc.scalar.copy(
                    out=y1_sorted[:].rearrange("n b (q r) -> n q b r", r=RUN),
                    in_=y1[:].rearrange("n (q b r) -> n q b r", b=PACK, r=RUN),
                )
            if step == Y_STEP + 1:
                y_turned = transpose_features(nc, psum_t, y1_sorted[:], ident)
            if step == Y_STEP + 2:
                y_grouped = group_features(nc, keep, y_turned, "y")
            if step == Y_STEP + 3:
                y_codes, y_scales = quantise_features(nc, keep, y_grouped, "y")
            for g in groups_ending_at(step - SECOND_LAG):
                second_product(g, 0, GROUP)
            for g in groups_ending_at(step - GATHER_LAG):
                if g < LATE_GATHER:
                    gather(nc.scalar.copy, g, slice(0, P))

        last = N_GROUPS - 1
        for g in range(LATE_GROUP, last):
            second_product(g, 0, GROUP)
        second_product(last, 0, GROUP // 2)
        second_product(last, GROUP // 2, GROUP // 2)

        y_chunk = P // STORE_CHUNKS
        for c in range(STORE_CHUNKS):
            ys = slice(c * y_chunk, (c + 1) * y_chunk)
            for g in range(LATE_GATHER, N_GROUPS):
                gather(nc.scalar.copy if g in (LATE_GATHER, last) else nc.vector.tensor_copy, g, ys)
            nc.sync.dma_start(out=out_rows[:, ys, :], in_=out_sb[:, ys, :])
